import numpy as np
import ml_dtypes


def mxq(x, axis, fmt="e4m3"):
    dtype, down = {"e4m3": (ml_dtypes.float8_e4m3fn, 7), "e5m2": (ml_dtypes.float8_e5m2, 14)}[fmt]
    v = np.moveaxis(np.asarray(x, np.float32).astype(ml_dtypes.bfloat16).astype(np.float64), axis, -1)
    blocks = v.reshape(v.shape[:-1] + (-1, 32))
    amax = np.abs(blocks).max(-1, keepdims=True)
    byte = np.maximum(np.where(amax > 0, np.frexp(amax)[1] - 1 + 127, 0) - down, 1)
    scale = np.exp2(byte - 127.0)
    codes = (blocks / scale).astype(np.float32).astype(dtype).astype(np.float64)
    return np.moveaxis((codes * scale).reshape(v.shape), -1, axis)


WIDE = False


def mx_kscale(k):
    if not WIDE:
        return np.ones(k)
    levels = np.array([10, -10, 5, -5, 0])
    if k % 512:
        return np.exp2(np.random.permutation(np.resize(levels, k // 32))).repeat(32)
    a = np.empty((k // 512, 16))
    for p in range(k // 512):
        a[p, :8] = np.random.permutation(np.resize(levels, 8))
        for g in range(8):
            far = levels[np.abs(levels - a[p, g]) >= 10]
            a[p, g + 8] = far[np.random.randint(len(far))]
    return np.exp2(a.ravel()).repeat(32)


BF16 = ml_dtypes.bfloat16


def bf(x):
    return np.asarray(x, np.float32).astype(BF16)


def f64(x):
    return np.asarray(x).astype(np.float64)


B, E, D, H = 256, 8, 128, 1024


def swish(v):
    with np.errstate(over="ignore"):
        return v / (1.0 + np.exp(-v))


def setup_inputs():
    a = mx_kscale(H)
    t = np.maximum(a, 1.0 / a) ** 2
    return {"u": bf(np.random.standard_normal((B * E, D))),
            "W1": bf(np.random.standard_normal((E, D, H)) * 1.5 / np.sqrt(D) * t),
            "b1": bf(np.random.standard_normal((E, H)) * 0.3 * t),
            "W2": bf(np.random.standard_normal((E, H, H)) * 1.5 / np.sqrt(H) / t[:, None]),
            "b2": bf(np.random.standard_normal((E, H)) * 0.3)}


def reference(u, W1, b1, W2, b2):
    x = f64(u).reshape(-1, E, D).transpose(1, 0, 2)
    h1 = swish(x @ f64(W1) + f64(b1)[:, None, :])
    h2 = swish((mxq(h1, 2, "e4m3") @ mxq(f64(W2), 1, "e4m3")) + f64(b2)[:, None, :])
    return h2.transpose(1, 0, 2)

@@ -1,0 +1,268 @@
+from contextlib import ExitStack
+
+import concourse.mybir as mybir
+from concourse.masks import make_identity
+
+BF16 = mybir.dt.bfloat16
+F32 = mybir.dt.float32
+U32 = mybir.dt.uint32
+U8 = mybir.dt.uint8
+FP8X4 = mybir.dt.float8_e4m3fn_x4
+SILU = mybir.ActivationFunctionType.Silu
+
+P = 128
+PACK = 4
+ENVS = 8
+BATCH = 256
+D_IN = 128
+HIDDEN = 1024
+K_PASS = P * PACK
+PASSES = HIDDEN // K_PASS
+B_ROWS = ENVS * PASSES
+ROW_SETS = BATCH // P
+HALF = 512
+HALVES = HIDDEN // HALF
+COLS = HALF // P
+STEPS = ENVS * HALVES
+RUN = 4
+LOAD_AHEAD = 3
+FIRST_AHEAD = 2
+ENVS_IN_BANK = 4
+H1_SCALAR_COLS = 128
+
+FLOPS = 2 * ENVS * BATCH * HIDDEN * (D_IN + HIDDEN)
+
+
+def tile_environvectorfield_pa_kernel(tc, u, W1, b1, W2, b2, out):
+    nc = tc.nc
+    with ExitStack() as ctx:
+        const = ctx.enter_context(tc.tile_pool(name="const", bufs=1))
+        raw_pool = ctx.enter_context(tc.tile_pool(name="raw", bufs=LOAD_AHEAD))
+        grouped_pool = ctx.enter_context(tc.tile_pool(name="grouped", bufs=3))
+        w2_mx_pool = ctx.enter_context(tc.tile_pool(name="w2_mx", bufs=3))
+        h1_pool = ctx.enter_context(tc.tile_pool(name="h1", bufs=3))
+        h1_mx_pool = ctx.enter_context(tc.tile_pool(name="h1_mx", bufs=3))
+        h2_pool = ctx.enter_context(tc.tile_pool(name="h2", bufs=3))
+        out_pool = ctx.enter_context(tc.tile_pool(name="out", bufs=4))
+        psum_setup = ctx.enter_context(tc.psum_pool(name="psum_setup", bufs=2))
+        psum_hidden = ctx.enter_context(tc.psum_pool(name="psum_hidden", bufs=2))
+        psum_mx = ctx.enter_context(tc.psum_pool(name="psum_mx", bufs=2))
+        psum_back = ctx.enter_context(tc.psum_pool(name="psum_back", bufs=2))
+        ctx.enter_context(tc.manual_schedule())
+
+        w1_sb = const.tile([P, ENVS, HIDDEN], BF16, name="w1_sb")
+        w2_raw = {}
+
+        def load_w1(e):
+            nc.sync.dma_start(out=w1_sb[:, e, :], in_=W1[e])
+
+        def load_w2(e, c):
+            if c == 0:
+                w2_raw[e] = raw_pool.tile([P, PASSES, PACK, HIDDEN], BF16, name="w2_raw")
+            rows = W2[e, c * K_PASS : (c + 1) * K_PASS, :]
+            nc.sync.dma_start(out=w2_raw[e][:, c, :, :], in_=rows.rearrange("(p t) n -> p t n", t=PACK))
+
+        def load_weights(e):
+            load_w1(e)
+            for c in range(PASSES):
+                load_w2(e, c)
+
+        load_w2(0, 0)
+        bias_rows = const.tile([P, K_PASS], BF16, name="bias_rows")
+        nc.gpsimd.memset(bias_rows[:], 0.0)
+        nc.sync.dma_start(out=bias_rows[0:B_ROWS, :], in_=b1.rearrange("e (c n) -> (e c) n", n=K_PASS))
+        nc.sync.dma_start(out=bias_rows[B_ROWS : 2 * B_ROWS, :], in_=b2.rearrange("e (c n) -> (e c) n", n=K_PASS))
+        u_sb = const.tile([P, ROW_SETS * ENVS, D_IN], BF16, name="u_sb")
+        nc.sync.dma_start(out=u_sb[:], in_=u.rearrange("(p i) d -> p i d", p=P))
+        load_w1(0)
+        load_w2(0, 1)
+        for e in range(1, LOAD_AHEAD):
+            load_weights(e)
+
+        ident_bf16 = const.tile([P, P], BF16, name="ident_bf16")
+        make_identity(nc, ident_bf16[:])
+        ident_f32 = const.tile([P, P], F32, name="ident_f32")
+        make_identity(nc, ident_f32[:])
+
+        bias_ps = psum_setup.tile([P, 2, PACK, P], BF16, name="bias_ps", tag="setup")
+        for t in range(PACK):
+            nc.tensor.transpose(out=bias_ps[:, 0, t, :], in_=bias_rows[:, t::PACK], identity=ident_bf16[:])
+        for col in range(COLS):
+            nc.tensor.transpose(
+                out=bias_ps[:, 1, col, :], in_=bias_rows[:, col * P : (col + 1) * P], identity=ident_bf16[:]
+            )
+        b1_cols = const.tile([P, PACK, B_ROWS], F32, name="b1_cols")
+        nc.scalar.copy(out=b1_cols[:], in_=bias_ps[:, 0, :, 0:B_ROWS])
+        b2_cols = const.tile([P, COLS, B_ROWS], F32, name="b2_cols")
+        nc.scalar.copy(out=b2_cols[:], in_=bias_ps[:, 1, :, B_ROWS : 2 * B_ROWS])
+
+        xT = const.tile([P, ENVS, ROW_SETS, P], BF16, name="xT")
+
+        def transpose_x(e0):
+            xT_ps = psum_setup.tile([P, ENVS_IN_BANK, ROW_SETS, P], BF16, name="xT_ps", tag="setup")
+            for e in range(ENVS_IN_BANK):
+                for s in range(ROW_SETS):
+                    nc.tensor.transpose(
+                        out=xT_ps[:, e, s, :], in_=u_sb[:, s * ENVS + e0 + e, :], identity=ident_bf16[:]
+                    )
+            nc.scalar.copy(out=xT[:, e0 : e0 + ENVS_IN_BANK, :, :], in_=xT_ps[:])
+
+        h1_bf16 = {}
+        h1_grouped = {}
+        h1_codes = {}
+        h1_scales = {}
+
+        def first_layer(e, c):
+            h1_bf16[e, c] = h1_pool.tile([P, PACK, BATCH], BF16, name="h1_bf16")
+            x_cols = xT[:, e, :, :].rearrange("d s p -> d (s p)")
+            for pair in range(PACK // 2):
+                acc = psum_hidden.tile([P, 2, BATCH], F32, name="hidden_acc")
+                for j in range(2):
+                    t = pair * 2 + j
+                    nc.tensor.matmul(
+                        out=acc[:, j, :],
+                        lhsT=w1_sb[:, e, c * K_PASS + t : (c + 1) * K_PASS : PACK],
+                        rhs=x_cols,
+                        start=True,
+                        stop=True,
+                    )
+                for j in range(2):
+                    t = pair * 2 + j
+                    row = e * PASSES + c
+                    nc.scalar.activation(
+                        out=h1_bf16[e, c][:, t, :],
+                        in_=acc[:, j, :],
+                        func=SILU,
+                        bias=b1_cols[:, t, row : row + 1],
+                    )
+
+        def regroup_h1(e, c):
+            h1_grouped[e, c] = h1_pool.tile([P, BATCH, PACK], BF16, name="h1_grouped", align_bytes=64)
+            split = BATCH - H1_SCALAR_COLS
+            nc.vector.tensor_copy(
+                out=h1_grouped[e, c][:, 0:split, :].rearrange("p (k i) t -> p k t i", i=RUN),
+                in_=h1_bf16[e, c][:, :, 0:split].rearrange("p t (k i) -> p k t i", i=RUN),
+            )
+            nc.scalar.copy(
+                out=h1_grouped[e, c][:, split:BATCH, :].rearrange("p (k i) t -> p k t i", i=RUN),
+                in_=h1_bf16[e, c][:, :, split:BATCH].rearrange("p t (k i) -> p k t i", i=RUN),
+            )
+
+        def quantise_h1(e, c):
+            if c == 0:
+                h1_codes[e] = h1_mx_pool.tile([P, PASSES, BATCH], U32, name="h1_codes", align_bytes=64)
+                h1_scales[e] = h1_mx_pool.tile([P, PASSES, BATCH], U8, name="h1_scales", align_bytes=64)
+            nc.vector.quantize_mx(
+                out=h1_codes[e][:, c, :].bitcast(FP8X4),
+                scales=h1_scales[e][:, c, :],
+                in_=h1_grouped[e, c][:].rearrange("p w t -> p (w t)"),
+            )
+
+        w2_grouped = {}
+        w2_codes = {}
+        w2_scales = {}
+
+        def regroup_w2(e, half, c0, c1):
+            if c0 == 0:
+                w2_grouped[e, half] = grouped_pool.tile(
+                    [P, PASSES, HALF, PACK], BF16, name="w2_grouped", align_bytes=64
+                )
+            nc.vector.tensor_copy(
+                out=w2_grouped[e, half][:, c0:c1, :, :].rearrange("p c (k i) t -> p c k t i", i=RUN),
+                in_=w2_raw[e][:, c0:c1, :, half * HALF : (half + 1) * HALF].rearrange(
+                    "p c t (k i) -> p c k t i", i=RUN
+                ),
+            )
+
+        def quantise_w2(e, half, c0, c1):
+            if c0 == 0:
+                w2_codes[e, half] = w2_mx_pool.tile([P, PASSES, HALF], U32, name="w2_codes", align_bytes=64)
+                w2_scales[e, half] = w2_mx_pool.tile([P, PASSES, HALF], U8, name="w2_scales", align_bytes=64)
+            nc.vector.quantize_mx(
+                out=w2_codes[e, half][:, c0:c1, :].rearrange("p c w -> p (c w)").bitcast(FP8X4),
+                scales=w2_scales[e, half][:, c0:c1, :].rearrange("p c w -> p (c w)"),
+                in_=w2_grouped[e, half][:, c0:c1, :, :].rearrange("p c w t -> p (c w t)"),
+            )
+
+        h2T = {}
+        h2_back = {}
+
+        def second_layer(e, half):
+            h2T[e, half] = h2_pool.tile([P, COLS, BATCH], F32, name="h2T")
+            for pair in range(COLS // 2):
+                acc = psum_mx.tile([P, 2, BATCH], F32, name="mx_acc")
+                for j in range(2):
+                    col = pair * 2 + j
+                    for c in range(PASSES):
+                        nc.tensor.matmul_mx(
+                            out=acc[:, j, :],
+                            lhsT=w2_codes[e, half][:, c, col * P : (col + 1) * P].bitcast(FP8X4),
+                            lhsT_scale=w2_scales[e, half][:, c, col * P : (col + 1) * P],
+                            rhs=h1_codes[e][:, c, :].bitcast(FP8X4),
+                            rhs_scale=h1_scales[e][:, c, :],
+                            start=(c == 0),
+                            stop=(c == PASSES - 1),
+                        )
+                for j in range(2):
+                    col = pair * 2 + j
+                    row = e * HALVES + half
+                    nc.scalar.activation(
+                        out=h2T[e, half][:, col, :],
+                        in_=acc[:, j, :],
+                        func=SILU,
+                        bias=b2_cols[:, col, row : row + 1],
+                    )
+
+        def transpose_back(e, half):
+            for s in range(ROW_SETS):
+                h2_back[e, half, s] = psum_back.tile([P, COLS, P], F32, name="h2_back")
+            for col in range(COLS):
+                for s in range(ROW_SETS):
+                    nc.tensor.transpose(
+                        out=h2_back[e, half, s][:, col, :],
+                        in_=h2T[e, half][:, col, s * P : (s + 1) * P],
+                        identity=ident_f32[:],
+                    )
+
+        out_rows = out.rearrange("(p s) e n -> p s e n", s=ROW_SETS)
+
+        def store(e, half, vector_is_free):
+            for s in range(ROW_SETS):
+                h2_sb = out_pool.tile([P, HALF], F32, name="h2_sb")
+                copy = nc.vector.tensor_copy if vector_is_free and s == ROW_SETS - 1 else nc.scalar.copy
+                copy(out=h2_sb[:], in_=h2_back[e, half, s][:].rearrange("p c n -> p (c n)"))
+                nc.sync.dma_start(out=out_rows[:, s, e, half * HALF : (half + 1) * HALF], in_=h2_sb[:])
+
+        for c in range(PASSES):
+            for half in range(HALVES):
+                regroup_w2(0, half, c, c + 1)
+            for half in range(HALVES):
+                quantise_w2(0, half, c, c + 1)
+        load_weights(LOAD_AHEAD)
+        transpose_x(0)
+        for first in range(FIRST_AHEAD + 1):
+            first_layer(*divmod(first, PASSES))
+            regroup_h1(*divmod(first, PASSES))
+        transpose_x(ENVS_IN_BANK)
+        for first in range(FIRST_AHEAD + 1):
+            quantise_h1(*divmod(first, PASSES))
+
+        for i in range(1, STEPS + 2):
+            if 0 <= i - 2:
+                store(*divmod(i - 2, HALVES), vector_is_free=(i >= STEPS))
+            if HALVES <= i < STEPS:
+                e, half = divmod(i, HALVES)
+                regroup_w2(e, half, 0, PASSES)
+                if i + 1 < STEPS:
+                    regroup_h1(*divmod(i + 1, PASSES))
+                quantise_w2(e, half, 0, PASSES)
+                if i + 1 < STEPS:
+                    quantise_h1(*divmod(i + 1, PASSES))
+                if half == HALVES - 1 and e + LOAD_AHEAD < ENVS:
+                    load_weights(e + LOAD_AHEAD)
+            if i - 1 < STEPS:
+                second_layer(*divmod(i - 1, HALVES))
+            if i + FIRST_AHEAD < STEPS:
+                first_layer(*divmod(i + FIRST_AHEAD, PASSES))
+            if i - 1 < STEPS:
+                transpose_back(*divmod(i - 1, HALVES))

@@ -25,7 +25,7 @@ HALVES = HIDDEN // HALF
 COLS = HALF // P
 STEPS = ENVS * HALVES
 RUN = 4
-LOAD_AHEAD = 3
+LOAD_AHEAD = 2
 FIRST_AHEAD = 2
 ENVS_IN_BANK = 4
 H1_SCALAR_COLS = 128
@@ -37,17 +37,16 @@ def tile_environvectorfield_pa_kernel(tc, u, W1, b1, W2, b2, out):
     nc = tc.nc
     with ExitStack() as ctx:
         const = ctx.enter_context(tc.tile_pool(name="const", bufs=1))
-        raw_pool = ctx.enter_context(tc.tile_pool(name="raw", bufs=LOAD_AHEAD))
+        raw_pool = ctx.enter_context(tc.tile_pool(name="raw", bufs=LOAD_AHEAD + 2))
         grouped_pool = ctx.enter_context(tc.tile_pool(name="grouped", bufs=3))
         w2_mx_pool = ctx.enter_context(tc.tile_pool(name="w2_mx", bufs=3))
         h1_pool = ctx.enter_context(tc.tile_pool(name="h1", bufs=3))
         h1_mx_pool = ctx.enter_context(tc.tile_pool(name="h1_mx", bufs=3))
         h2_pool = ctx.enter_context(tc.tile_pool(name="h2", bufs=3))
-        out_pool = ctx.enter_context(tc.tile_pool(name="out", bufs=4))
-        psum_setup = ctx.enter_context(tc.psum_pool(name="psum_setup", bufs=2))
+        out_pool = ctx.enter_context(tc.tile_pool(name="out", bufs=6))
         psum_hidden = ctx.enter_context(tc.psum_pool(name="psum_hidden", bufs=2))
-        psum_mx = ctx.enter_context(tc.psum_pool(name="psum_mx", bufs=2))
-        psum_back = ctx.enter_context(tc.psum_pool(name="psum_back", bufs=2))
+        psum_mx = ctx.enter_context(tc.psum_pool(name="psum_mx", bufs=3))
+        psum_back = ctx.enter_context(tc.psum_pool(name="psum_back", bufs=3))
         ctx.enter_context(tc.manual_schedule())
 
         w1_sb = const.tile([P, ENVS, HIDDEN], BF16, name="w1_sb")
@@ -56,35 +55,50 @@ def tile_environvectorfield_pa_kernel(tc, u, W1, b1, W2, b2, out):
         def load_w1(e):
             nc.sync.dma_start(out=w1_sb[:, e, :], in_=W1[e])
 
+        def w2_rows(e, c):
+            return W2[e, c * K_PASS : (c + 1) * K_PASS, :].rearrange("(p t) n -> p t n", t=PACK)
+
         def load_w2(e, c):
             if c == 0:
                 w2_raw[e] = raw_pool.tile([P, PASSES, PACK, HIDDEN], BF16, name="w2_raw")
-            rows = W2[e, c * K_PASS : (c + 1) * K_PASS, :]
-            nc.sync.dma_start(out=w2_raw[e][:, c, :, :], in_=rows.rearrange("(p t) n -> p t n", t=PACK))
+            nc.sync.dma_start(out=w2_raw[e][:, c, :, :], in_=w2_rows(e, c))
 
-        def load_weights(e):
-            load_w1(e)
-            for c in range(PASSES):
-                load_w2(e, c)
+        w2_start = [const.tile([P, PACK, HALF], BF16, name="w2_start_%d" % half) for half in range(HALVES)]
+        w2_second = const.tile([P, PACK, HIDDEN], BF16, name="w2_second")
+        u_rows = u.rearrange("(p s e) d -> p s e d", s=ROW_SETS, e=ENVS)
+        u_sb = [
+            const.tile([P, ROW_SETS, ENVS_IN_BANK, D_IN], BF16, name="u_sb_%d" % g) for g in range(ENVS // ENVS_IN_BANK)
+        ]
 
-        load_w2(0, 0)
+        def load_u(g):
+            nc.sync.dma_start(out=u_sb[g][:], in_=u_rows[:, :, g * ENVS_IN_BANK : (g + 1) * ENVS_IN_BANK, :])
+
+        def load_start(half):
+            nc.sync.dma_start(out=w2_start[half][:], in_=w2_rows(0, 0)[:, :, half * HALF : (half + 1) * HALF])
+
         bias_rows = const.tile([P, K_PASS], BF16, name="bias_rows")
         nc.gpsimd.memset(bias_rows[:], 0.0)
+        load_start(0)
         nc.sync.dma_start(out=bias_rows[0:B_ROWS, :], in_=b1.rearrange("e (c n) -> (e c) n", n=K_PASS))
         nc.sync.dma_start(out=bias_rows[B_ROWS : 2 * B_ROWS, :], in_=b2.rearrange("e (c n) -> (e c) n", n=K_PASS))
-        u_sb = const.tile([P, ROW_SETS * ENVS, D_IN], BF16, name="u_sb")
-        nc.sync.dma_start(out=u_sb[:], in_=u.rearrange("(p i) d -> p i d", p=P))
+        load_u(0)
+        load_start(1)
         load_w1(0)
-        load_w2(0, 1)
-        for e in range(1, LOAD_AHEAD):
-            load_weights(e)
+        nc.sync.dma_start(out=w2_second[:], in_=w2_rows(0, 1))
+        load_w1(1)
+        load_w2(1, 0)
+        load_u(1)
+        load_w2(1, 1)
+        for c in range(PASSES):
+            load_w2(2, c)
+        load_w1(2)
 
         ident_bf16 = const.tile([P, P], BF16, name="ident_bf16")
         make_identity(nc, ident_bf16[:])
         ident_f32 = const.tile([P, P], F32, name="ident_f32")
         make_identity(nc, ident_f32[:])
 
-        bias_ps = psum_setup.tile([P, 2, PACK, P], BF16, name="bias_ps", tag="setup")
+        bias_ps = psum_back.tile([P, 2, PACK, P], BF16, name="bias_ps", tag="back")
         for t in range(PACK):
             nc.tensor.transpose(out=bias_ps[:, 0, t, :], in_=bias_rows[:, t::PACK], identity=ident_bf16[:])
         for col in range(COLS):
@@ -93,42 +107,46 @@ def tile_environvectorfield_pa_kernel(tc, u, W1, b1, W2, b2, out):
             )
         b1_cols = const.tile([P, PACK, B_ROWS], F32, name="b1_cols")
         nc.scalar.copy(out=b1_cols[:], in_=bias_ps[:, 0, :, 0:B_ROWS])
+        b1_bf16 = const.tile([P, PACK, B_ROWS], BF16, name="b1_bf16")
+        nc.scalar.copy(out=b1_bf16[:], in_=bias_ps[:, 0, :, 0:B_ROWS])
         b2_cols = const.tile([P, COLS, B_ROWS], F32, name="b2_cols")
         nc.scalar.copy(out=b2_cols[:], in_=bias_ps[:, 1, :, B_ROWS : 2 * B_ROWS])
 
         xT = const.tile([P, ENVS, ROW_SETS, P], BF16, name="xT")
 
-        def transpose_x(e0):
-            xT_ps = psum_setup.tile([P, ENVS_IN_BANK, ROW_SETS, P], BF16, name="xT_ps", tag="setup")
+        def transpose_x(g):
+            xT_ps = psum_back.tile([P, ENVS_IN_BANK, ROW_SETS, P], BF16, name="xT_ps", tag="back")
             for e in range(ENVS_IN_BANK):
                 for s in range(ROW_SETS):
-                    nc.tensor.transpose(
-                        out=xT_ps[:, e, s, :], in_=u_sb[:, s * ENVS + e0 + e, :], identity=ident_bf16[:]
-                    )
-            nc.scalar.copy(out=xT[:, e0 : e0 + ENVS_IN_BANK, :, :], in_=xT_ps[:])
+                    nc.tensor.transpose(out=xT_ps[:, e, s, :], in_=u_sb[g][:, s, e, :], identity=ident_bf16[:])
+            nc.scalar.copy(out=xT[:, g * ENVS_IN_BANK : (g + 1) * ENVS_IN_BANK, :, :], in_=xT_ps[:])
 
         h1_bf16 = {}
         h1_grouped = {}
         h1_codes = {}
         h1_scales = {}
 
+        def w1_columns(e, c, t):
+            return w1_sb[:, e, c * K_PASS + t : (c + 1) * K_PASS : PACK]
+
         def first_layer(e, c):
+            if c == 0:
+                first_layer_biased(e, c)
+            else:
+                first_layer_grouped(e, c)
+
+        def first_layer_biased(e, c):
             h1_bf16[e, c] = h1_pool.tile([P, PACK, BATCH], BF16, name="h1_bf16")
             x_cols = xT[:, e, :, :].rearrange("d s p -> d (s p)")
+            row = e * PASSES + c
             for pair in range(PACK // 2):
                 acc = psum_hidden.tile([P, 2, BATCH], F32, name="hidden_acc")
                 for j in range(2):
-                    t = pair * 2 + j
                     nc.tensor.matmul(
-                        out=acc[:, j, :],
-                        lhsT=w1_sb[:, e, c * K_PASS + t : (c + 1) * K_PASS : PACK],
-                        rhs=x_cols,
-                        start=True,
-                        stop=True,
+                        out=acc[:, j, :], lhsT=w1_columns(e, c, pair * 2 + j), rhs=x_cols, start=True, stop=True
                     )
                 for j in range(2):
                     t = pair * 2 + j
-                    row = e * PASSES + c
                     nc.scalar.activation(
                         out=h1_bf16[e, c][:, t, :],
                         in_=acc[:, j, :],
@@ -136,17 +154,44 @@ def tile_environvectorfield_pa_kernel(tc, u, W1, b1, W2, b2, out):
                         bias=b1_cols[:, t, row : row + 1],
                     )
 
-        def regroup_h1(e, c):
+        def first_layer_grouped(e, c):
             h1_grouped[e, c] = h1_pool.tile([P, BATCH, PACK], BF16, name="h1_grouped", align_bytes=64)
+            row = e * PASSES + c
+            for s in range(ROW_SETS):
+                acc = psum_hidden.tile([P, PACK, P], F32, name="hidden_acc")
+                for t in range(PACK):
+                    nc.tensor.matmul(
+                        out=acc[:, t, :],
+                        lhsT=ident_bf16[:],
+                        rhs=b1_bf16[:, t, row : row + 1].to_broadcast([P, P]),
+                        start=True,
+                        stop=False,
+                    )
+                    nc.tensor.matmul(
+                        out=acc[:, t, :], lhsT=w1_columns(e, c, t), rhs=xT[:, e, s, :], start=False, stop=True
+                    )
+                nc.scalar.activation(
+                    out=h1_grouped[e, c][:, s * P : (s + 1) * P, :],
+                    in_=acc[:].rearrange("p t n -> p n t"),
+                    func=SILU,
+                )
+
+        def regroup_h1(e, c, vector=True, scalar=True):
+            if c != 0:
+                return
+            if scalar:
+                h1_grouped[e, c] = h1_pool.tile([P, BATCH, PACK], BF16, name="h1_grouped", align_bytes=64)
             split = BATCH - H1_SCALAR_COLS
-            nc.vector.tensor_copy(
-                out=h1_grouped[e, c][:, 0:split, :].rearrange("p (k i) t -> p k t i", i=RUN),
-                in_=h1_bf16[e, c][:, :, 0:split].rearrange("p t (k i) -> p k t i", i=RUN),
-            )
-            nc.scalar.copy(
-                out=h1_grouped[e, c][:, split:BATCH, :].rearrange("p (k i) t -> p k t i", i=RUN),
-                in_=h1_bf16[e, c][:, :, split:BATCH].rearrange("p t (k i) -> p k t i", i=RUN),
-            )
+            shares = []
+            if vector:
+                shares.append((nc.vector.tensor_copy, 0, split))
+            if scalar:
+                shares.append((nc.scalar.copy, split, BATCH))
+            for copy, n0, n1 in shares:
+                copy(
+                    out=h1_grouped[e, c][:, n0:n1, :].rearrange("p (k i) t -> p k t i", i=RUN),
+                    in_=h1_bf16[e, c][:, :, n0:n1].rearrange("p t (k i) -> p k t i", i=RUN),
+                )
 
         def quantise_h1(e, c):
             if c == 0:
@@ -162,19 +207,23 @@ def tile_environvectorfield_pa_kernel(tc, u, W1, b1, W2, b2, out):
         w2_codes = {}
         w2_scales = {}
 
-        def regroup_w2(e, half, c0, c1):
-            if c0 == 0:
-                w2_grouped[e, half] = grouped_pool.tile(
-                    [P, PASSES, HALF, PACK], BF16, name="w2_grouped", align_bytes=64
-                )
-            nc.vector.tensor_copy(
-                out=w2_grouped[e, half][:, c0:c1, :, :].rearrange("p c (k i) t -> p c k t i", i=RUN),
-                in_=w2_raw[e][:, c0:c1, :, half * HALF : (half + 1) * HALF].rearrange(
-                    "p c t (k i) -> p c k t i", i=RUN
-                ),
-            )
+        def regroup_copy(dst, src):
+            if len(dst.shape) == 3:
+                dst = dst.rearrange("p (k i) t -> p k t i", i=RUN)
+                src = src.rearrange("p t (k i) -> p k t i", i=RUN)
+            else:
+                dst = dst.rearrange("p c (k i) t -> p c k t i", i=RUN)
+                src = src.rearrange("p c t (k i) -> p c k t i", i=RUN)
+            nc.vector.tensor_copy(out=dst, in_=src)
 
-        def quantise_w2(e, half, c0, c1):
+        def new_grouped(e, half):
+            w2_grouped[e, half] = grouped_pool.tile([P, PASSES, HALF, PACK], BF16, name="w2_grouped", align_bytes=64)
+
+        def regroup_w2(e, half):
+            new_grouped(e, half)
+            regroup_copy(w2_grouped[e, half][:], w2_raw[e][:, :, :, half * HALF : (half + 1) * HALF])
+
+        def quantise_w2(e, half, c0=0, c1=PASSES):
             if c0 == 0:
                 w2_codes[e, half] = w2_mx_pool.tile([P, PASSES, HALF], U32, name="w2_codes", align_bytes=64)
                 w2_scales[e, half] = w2_mx_pool.tile([P, PASSES, HALF], U8, name="w2_scales", align_bytes=64)
@@ -215,7 +264,7 @@ def tile_environvectorfield_pa_kernel(tc, u, W1, b1, W2, b2, out):
 
         def transpose_back(e, half):
             for s in range(ROW_SETS):
-                h2_back[e, half, s] = psum_back.tile([P, COLS, P], F32, name="h2_back")
+                h2_back[e, half, s] = psum_back.tile([P, COLS, P], F32, name="h2_back", tag="back")
             for col in range(COLS):
                 for s in range(ROW_SETS):
                     nc.tensor.transpose(
@@ -226,40 +275,51 @@ def tile_environvectorfield_pa_kernel(tc, u, W1, b1, W2, b2, out):
 
         out_rows = out.rearrange("(p s) e n -> p s e n", s=ROW_SETS)
 
-        def store(e, half, vector_is_free):
+        def store(e, half, on_vector):
             for s in range(ROW_SETS):
                 h2_sb = out_pool.tile([P, HALF], F32, name="h2_sb")
-                copy = nc.vector.tensor_copy if vector_is_free and s == ROW_SETS - 1 else nc.scalar.copy
+                copy = nc.vector.tensor_copy if s in on_vector else nc.scalar.copy
                 copy(out=h2_sb[:], in_=h2_back[e, half, s][:].rearrange("p c n -> p (c n)"))
                 nc.sync.dma_start(out=out_rows[:, s, e, half * HALF : (half + 1) * HALF], in_=h2_sb[:])
 
-        for c in range(PASSES):
-            for half in range(HALVES):
-                regroup_w2(0, half, c, c + 1)
-            for half in range(HALVES):
-                quantise_w2(0, half, c, c + 1)
-        load_weights(LOAD_AHEAD)
+        for half in range(HALVES):
+            new_grouped(0, half)
+        regroup_copy(w2_grouped[0, 0][:, 0, :, :], w2_start[0][:])
+        quantise_w2(0, 0, 0, 1)
+        regroup_copy(w2_grouped[0, 1][:, 0, :, :], w2_start[1][:])
+        regroup_copy(w2_grouped[0, 0][:, 1, :, :], w2_second[:, :, 0:HALF])
+        quantise_w2(0, 1, 0, 1)
+        regroup_copy(w2_grouped[0, 1][:, 1, :, :], w2_second[:, :, HALF:HIDDEN])
+        quantise_w2(0, 0, 1, 2)
+        quantise_w2(0, 1, 1, 2)
         transpose_x(0)
         for first in range(FIRST_AHEAD + 1):
             first_layer(*divmod(first, PASSES))
-            regroup_h1(*divmod(first, PASSES))
-        transpose_x(ENVS_IN_BANK)
-        for first in range(FIRST_AHEAD + 1):
+            regroup_h1(*divmod(first, PASSES), vector=(first < FIRST_AHEAD))
+        transpose_x(1)
+        for first in range(FIRST_AHEAD):
             quantise_h1(*divmod(first, PASSES))
 
         for i in range(1, STEPS + 2):
+            e, half = divmod(i, HALVES)
+            if HALVES <= i and e + LOAD_AHEAD < ENVS:
+                load_w2(e + LOAD_AHEAD, half)
+                if half == 0:
+                    load_w1(e + LOAD_AHEAD)
             if 0 <= i - 2:
-                store(*divmod(i - 2, HALVES), vector_is_free=(i >= STEPS))
+                store(*divmod(i - 2, HALVES), on_vector={STEPS: (0, 1), STEPS + 1: (1,)}.get(i, ()))
             if HALVES <= i < STEPS:
-                e, half = divmod(i, HALVES)
-                regroup_w2(e, half, 0, PASSES)
+                regroup_w2(e, half)
+                if i == FIRST_AHEAD:
+                    regroup_h1(*divmod(i, PASSES), scalar=False)
+                    quantise_h1(*divmod(i, PASSES))
                 if i + 1 < STEPS:
                     regroup_h1(*divmod(i + 1, PASSES))
-                quantise_w2(e, half, 0, PASSES)
-                if i + 1 < STEPS:
+                    if half == 0:
+                        quantise_h1(*divmod(i + 1, PASSES))
+                quantise_w2(e, half)
+                if i + 1 < STEPS and half == 1:
                     quantise_h1(*divmod(i + 1, PASSES))
-                if half == HALVES - 1 and e + LOAD_AHEAD < ENVS:
-                    load_weights(e + LOAD_AHEAD)
             if i - 1 < STEPS:
                 second_layer(*divmod(i - 1, HALVES))
             if i + FIRST_AHEAD < STEPS:

@@ -24,7 +24,7 @@ HALF = 512
 HALVES = HIDDEN // HALF
 COLS = HALF // P
 STEPS = ENVS * HALVES
-RUN = 4
+RUN = 8
 LOAD_AHEAD = 2
 FIRST_AHEAD = 2
 ENVS_IN_BANK = 4

@@ -26,7 +26,8 @@ COLS = HALF // P
 STEPS = ENVS * HALVES
 RUN = 8
 LOAD_AHEAD = 2
-FIRST_AHEAD = 2
+LAST_PIECES = 2
+FIRST_AHEAD = 3
 ENVS_IN_BANK = 4
 H1_SCALAR_COLS = 128
 
@@ -40,13 +41,13 @@ def tile_environvectorfield_pa_kernel(tc, u, W1, b1, W2, b2, out):
         raw_pool = ctx.enter_context(tc.tile_pool(name="raw", bufs=LOAD_AHEAD + 2))
         grouped_pool = ctx.enter_context(tc.tile_pool(name="grouped", bufs=3))
         w2_mx_pool = ctx.enter_context(tc.tile_pool(name="w2_mx", bufs=3))
-        h1_pool = ctx.enter_context(tc.tile_pool(name="h1", bufs=3))
+        h1_pool = ctx.enter_context(tc.tile_pool(name="h1", bufs=4))
         h1_mx_pool = ctx.enter_context(tc.tile_pool(name="h1_mx", bufs=3))
         h2_pool = ctx.enter_context(tc.tile_pool(name="h2", bufs=3))
         out_pool = ctx.enter_context(tc.tile_pool(name="out", bufs=6))
         psum_hidden = ctx.enter_context(tc.psum_pool(name="psum_hidden", bufs=2))
-        psum_mx = ctx.enter_context(tc.psum_pool(name="psum_mx", bufs=3))
-        psum_back = ctx.enter_context(tc.psum_pool(name="psum_back", bufs=3))
+        psum_mx = ctx.enter_context(tc.psum_pool(name="psum_mx", bufs=2))
+        psum_back = ctx.enter_context(tc.psum_pool(name="psum_back", bufs=4))
         ctx.enter_context(tc.manual_schedule())
 
         w1_sb = const.tile([P, ENVS, HIDDEN], BF16, name="w1_sb")
@@ -63,8 +64,8 @@ def tile_environvectorfield_pa_kernel(tc, u, W1, b1, W2, b2, out):
                 w2_raw[e] = raw_pool.tile([P, PASSES, PACK, HIDDEN], BF16, name="w2_raw")
             nc.sync.dma_start(out=w2_raw[e][:, c, :, :], in_=w2_rows(e, c))
 
-        w2_start = [const.tile([P, PACK, HALF], BF16, name="w2_start_%d" % half) for half in range(HALVES)]
-        w2_second = const.tile([P, PACK, HIDDEN], BF16, name="w2_second")
+        start_pieces = [(0, 0, HALF), (0, HALF, HALF), (1, 0, HIDDEN)]
+        w2_start = [const.tile([P, PACK, w], BF16, name="w2_start_%d_%d" % (c, n0)) for c, n0, w in start_pieces]
         u_rows = u.rearrange("(p s e) d -> p s e d", s=ROW_SETS, e=ENVS)
         u_sb = [
             const.tile([P, ROW_SETS, ENVS_IN_BANK, D_IN], BF16, name="u_sb_%d" % g) for g in range(ENVS // ENVS_IN_BANK)
@@ -73,53 +74,68 @@ def tile_environvectorfield_pa_kernel(tc, u, W1, b1, W2, b2, out):
         def load_u(g):
             nc.sync.dma_start(out=u_sb[g][:], in_=u_rows[:, :, g * ENVS_IN_BANK : (g + 1) * ENVS_IN_BANK, :])
 
-        def load_start(half):
-            nc.sync.dma_start(out=w2_start[half][:], in_=w2_rows(0, 0)[:, :, half * HALF : (half + 1) * HALF])
+        def load_start(i):
+            c, n0, width = start_pieces[i]
+            nc.sync.dma_start(out=w2_start[i][:], in_=w2_rows(0, c)[:, :, n0 : n0 + width])
 
         bias_rows = const.tile([P, K_PASS], BF16, name="bias_rows")
         nc.gpsimd.memset(bias_rows[:], 0.0)
         load_start(0)
+        load_u(0)
         nc.sync.dma_start(out=bias_rows[0:B_ROWS, :], in_=b1.rearrange("e (c n) -> (e c) n", n=K_PASS))
         nc.sync.dma_start(out=bias_rows[B_ROWS : 2 * B_ROWS, :], in_=b2.rearrange("e (c n) -> (e c) n", n=K_PASS))
-        load_u(0)
-        load_start(1)
         load_w1(0)
-        nc.sync.dma_start(out=w2_second[:], in_=w2_rows(0, 1))
+        load_start(1)
+        load_start(2)
         load_w1(1)
         load_w2(1, 0)
-        load_u(1)
+        load_w1(2)
         load_w2(1, 1)
+        load_u(1)
+        load_w1(3)
         for c in range(PASSES):
             load_w2(2, c)
-        load_w1(2)
+
+        warm = const.tile([P, 1], F32, name="warm")
+        nc.vector.memset(warm[:], 0.0)
+        nc.scalar.activation(out=warm[:], in_=warm[:], func=SILU)
 
         ident_bf16 = const.tile([P, P], BF16, name="ident_bf16")
         make_identity(nc, ident_bf16[:])
         ident_f32 = const.tile([P, P], F32, name="ident_f32")
         make_identity(nc, ident_f32[:])
 
-        bias_ps = psum_back.tile([P, 2, PACK, P], BF16, name="bias_ps", tag="back")
-        for t in range(PACK):
-            nc.tensor.transpose(out=bias_ps[:, 0, t, :], in_=bias_rows[:, t::PACK], identity=ident_bf16[:])
-        for col in range(COLS):
-            nc.tensor.transpose(
-                out=bias_ps[:, 1, col, :], in_=bias_rows[:, col * P : (col + 1) * P], identity=ident_bf16[:]
-            )
         b1_cols = const.tile([P, PACK, B_ROWS], F32, name="b1_cols")
-        nc.scalar.copy(out=b1_cols[:], in_=bias_ps[:, 0, :, 0:B_ROWS])
         b1_bf16 = const.tile([P, PACK, B_ROWS], BF16, name="b1_bf16")
-        nc.scalar.copy(out=b1_bf16[:], in_=bias_ps[:, 0, :, 0:B_ROWS])
         b2_cols = const.tile([P, COLS, B_ROWS], F32, name="b2_cols")
-        nc.scalar.copy(out=b2_cols[:], in_=bias_ps[:, 1, :, B_ROWS : 2 * B_ROWS])
+
+        def transpose_b1():
+            b1_ps = psum_back.tile([P, PACK, P], BF16, name="b1_ps", tag="back")
+            for t in range(PACK):
+                nc.tensor.transpose(out=b1_ps[:, t, :], in_=bias_rows[:, t::PACK], identity=ident_bf16[:])
+            nc.scalar.copy(out=b1_cols[:], in_=b1_ps[:, :, 0:B_ROWS])
+            nc.scalar.copy(out=b1_bf16[:], in_=b1_ps[:, :, 0:B_ROWS])
+
+        def transpose_b2():
+            b2_ps = psum_back.tile([P, COLS, P], BF16, name="b2_ps", tag="back")
+            for col in range(COLS):
+                nc.tensor.transpose(
+                    out=b2_ps[:, col, :], in_=bias_rows[:, col * P : (col + 1) * P], identity=ident_bf16[:]
+                )
+            nc.scalar.copy(out=b2_cols[:], in_=b2_ps[:, :, B_ROWS : 2 * B_ROWS])
 
         xT = const.tile([P, ENVS, ROW_SETS, P], BF16, name="xT")
 
-        def transpose_x(g):
+        def transpose_x(e0, e1):
             xT_ps = psum_back.tile([P, ENVS_IN_BANK, ROW_SETS, P], BF16, name="xT_ps", tag="back")
-            for e in range(ENVS_IN_BANK):
+            for e in range(e0, e1):
                 for s in range(ROW_SETS):
-                    nc.tensor.transpose(out=xT_ps[:, e, s, :], in_=u_sb[g][:, s, e, :], identity=ident_bf16[:])
-            nc.scalar.copy(out=xT[:, g * ENVS_IN_BANK : (g + 1) * ENVS_IN_BANK, :, :], in_=xT_ps[:])
+                    nc.tensor.transpose(
+                        out=xT_ps[:, e - e0, s, :],
+                        in_=u_sb[e // ENVS_IN_BANK][:, s, e % ENVS_IN_BANK, :],
+                        identity=ident_bf16[:],
+                    )
+            nc.scalar.copy(out=xT[:, e0:e1, :, :], in_=xT_ps[:, 0 : e1 - e0, :, :])
 
         h1_bf16 = {}
         h1_grouped = {}
@@ -129,52 +145,56 @@ def tile_environvectorfield_pa_kernel(tc, u, W1, b1, W2, b2, out):
         def w1_columns(e, c, t):
             return w1_sb[:, e, c * K_PASS + t : (c + 1) * K_PASS : PACK]
 
-        def first_layer(e, c):
+        hidden_acc = {}
+
+        def first_matmuls(e, c):
+            row = e * PASSES + c
+            for bank in range(2):
+                if c == 0:
+                    acc = psum_hidden.tile([P, 2, BATCH], F32, name="hidden_acc")
+                    x_cols = xT[:, e, :, :].rearrange("d s p -> d (s p)")
+                    for j in range(2):
+                        nc.tensor.matmul(
+                            out=acc[:, j, :], lhsT=w1_columns(e, c, bank * 2 + j), rhs=x_cols, start=True, stop=True
+                        )
+                else:
+                    acc = psum_hidden.tile([P, PACK, P], F32, name="hidden_acc")
+                    for t in range(PACK):
+                        nc.tensor.matmul(
+                            out=acc[:, t, :],
+                            lhsT=ident_bf16[:],
+                            rhs=b1_bf16[:, t, row : row + 1].to_broadcast([P, P]),
+                            start=True,
+                            stop=False,
+                        )
+                        nc.tensor.matmul(
+                            out=acc[:, t, :], lhsT=w1_columns(e, c, t), rhs=xT[:, e, bank, :], start=False, stop=True
+                        )
+                hidden_acc[e, c, bank] = acc
+
+        def first_swish(e, c):
+            row = e * PASSES + c
             if c == 0:
-                first_layer_biased(e, c)
+                h1_bf16[e, c] = h1_pool.tile([P, PACK, BATCH], BF16, name="h1_bf16")
             else:
-                first_layer_grouped(e, c)
-
-        def first_layer_biased(e, c):
-            h1_bf16[e, c] = h1_pool.tile([P, PACK, BATCH], BF16, name="h1_bf16")
-            x_cols = xT[:, e, :, :].rearrange("d s p -> d (s p)")
-            row = e * PASSES + c
-            for pair in range(PACK // 2):
-                acc = psum_hidden.tile([P, 2, BATCH], F32, name="hidden_acc")
-                for j in range(2):
-                    nc.tensor.matmul(
-                        out=acc[:, j, :], lhsT=w1_columns(e, c, pair * 2 + j), rhs=x_cols, start=True, stop=True
-                    )
-                for j in range(2):
-                    t = pair * 2 + j
+                h1_grouped[e, c] = h1_pool.tile([P, BATCH, PACK], BF16, name="h1_grouped", align_bytes=64)
+            for bank in range(2):
+                acc = hidden_acc[e, c, bank]
+                if c == 0:
+                    for j in range(2):
+                        t = bank * 2 + j
+                        nc.scalar.activation(
+                            out=h1_bf16[e, c][:, t, :],
+                            in_=acc[:, j, :],
+                            func=SILU,
+                            bias=b1_cols[:, t, row : row + 1],
+                        )
+                else:
                     nc.scalar.activation(
-                        out=h1_bf16[e, c][:, t, :],
-                        in_=acc[:, j, :],
+                        out=h1_grouped[e, c][:, bank * P : (bank + 1) * P, :],
+                        in_=acc[:].rearrange("p t n -> p n t"),
                         func=SILU,
-                        bias=b1_cols[:, t, row : row + 1],
                     )
-
-        def first_layer_grouped(e, c):
-            h1_grouped[e, c] = h1_pool.tile([P, BATCH, PACK], BF16, name="h1_grouped", align_bytes=64)
-            row = e * PASSES + c
-            for s in range(ROW_SETS):
-                acc = psum_hidden.tile([P, PACK, P], F32, name="hidden_acc")
-                for t in range(PACK):
-                    nc.tensor.matmul(
-                        out=acc[:, t, :],
-                        lhsT=ident_bf16[:],
-                        rhs=b1_bf16[:, t, row : row + 1].to_broadcast([P, P]),
-                        start=True,
-                        stop=False,
-                    )
-                    nc.tensor.matmul(
-                        out=acc[:, t, :], lhsT=w1_columns(e, c, t), rhs=xT[:, e, s, :], start=False, stop=True
-                    )
-                nc.scalar.activation(
-                    out=h1_grouped[e, c][:, s * P : (s + 1) * P, :],
-                    in_=acc[:].rearrange("p t n -> p n t"),
-                    func=SILU,
-                )
 
         def regroup_h1(e, c, vector=True, scalar=True):
             if c != 0:
@@ -216,51 +236,80 @@ def tile_environvectorfield_pa_kernel(tc, u, W1, b1, W2, b2, out):
                 src = src.rearrange("p c t (k i) -> p c k t i", i=RUN)
             nc.vector.tensor_copy(out=dst, in_=src)
 
-        def new_grouped(e, half):
-            w2_grouped[e, half] = grouped_pool.tile([P, PASSES, HALF, PACK], BF16, name="w2_grouped", align_bytes=64)
+        def new_grouped(e, n0, width=HALF):
+            w2_grouped[e, n0] = grouped_pool.tile([P, PASSES, width, PACK], BF16, name="w2_grouped", align_bytes=64)
 
-        def regroup_w2(e, half):
-            new_grouped(e, half)
-            regroup_copy(w2_grouped[e, half][:], w2_raw[e][:, :, :, half * HALF : (half + 1) * HALF])
+        def regroup_w2(e, n0, width=HALF):
+            new_grouped(e, n0, width)
+            regroup_copy(w2_grouped[e, n0][:], w2_raw[e][:, :, :, n0 : n0 + width])
 
-        def quantise_w2(e, half, c0=0, c1=PASSES):
-            if c0 == 0:
-                w2_codes[e, half] = w2_mx_pool.tile([P, PASSES, HALF], U32, name="w2_codes", align_bytes=64)
-                w2_scales[e, half] = w2_mx_pool.tile([P, PASSES, HALF], U8, name="w2_scales", align_bytes=64)
+        def new_mx(e, n0, width=HALF):
+            w2_codes[e, n0] = w2_mx_pool.tile([P, PASSES, width], U32, name="w2_codes", align_bytes=64)
+            w2_scales[e, n0] = w2_mx_pool.tile([P, PASSES, width], U8, name="w2_scales", align_bytes=64)
+
+        def quantise_w2(e, n0, width=HALF):
+            new_mx(e, n0, width)
             nc.vector.quantize_mx(
-                out=w2_codes[e, half][:, c0:c1, :].rearrange("p c w -> p (c w)").bitcast(FP8X4),
-                scales=w2_scales[e, half][:, c0:c1, :].rearrange("p c w -> p (c w)"),
-                in_=w2_grouped[e, half][:, c0:c1, :, :].rearrange("p c w t -> p (c w t)"),
+                out=w2_codes[e, n0][:].rearrange("p c w -> p (c w)").bitcast(FP8X4),
+                scales=w2_scales[e, n0][:].rearrange("p c w -> p (c w)"),
+                in_=w2_grouped[e, n0][:].rearrange("p c w t -> p (c w t)"),
             )
+
+        def regroup_start(c, half):
+            if c == 0:
+                src = w2_start[half][:]
+            else:
+                src = w2_start[HALVES][:, :, half * HALF : (half + 1) * HALF]
+            regroup_copy(w2_grouped[0, half * HALF][:, c, :, :], src)
+
+        def quantise_start(c, half):
+            nc.vector.quantize_mx(
+                out=w2_codes[0, half * HALF][:, c, :].bitcast(FP8X4),
+                scales=w2_scales[0, half * HALF][:, c, :],
+                in_=w2_grouped[0, half * HALF][:, c, :, :].rearrange("p w t -> p (w t)"),
+            )
+
+        def pieces(e, half):
+            count = LAST_PIECES if (e, half) == (ENVS - 1, HALVES - 1) else 1
+            width = HALF // count
+            return [(half * HALF + i * width, width) for i in range(count)]
 
         h2T = {}
         h2_back = {}
 
-        def second_layer(e, half):
-            h2T[e, half] = h2_pool.tile([P, COLS, BATCH], F32, name="h2T")
+        mx_acc = {}
+
+        def second_matmuls(e, half):
+            stationary = []
+            for n0, width in pieces(e, half):
+                for m0 in range(0, width, P):
+                    stationary.append((w2_codes[e, n0], w2_scales[e, n0], slice(m0, m0 + P)))
             for pair in range(COLS // 2):
                 acc = psum_mx.tile([P, 2, BATCH], F32, name="mx_acc")
+                mx_acc[e, half, pair] = acc
                 for j in range(2):
-                    col = pair * 2 + j
+                    codes, scales, m = stationary[pair * 2 + j]
                     for c in range(PASSES):
                         nc.tensor.matmul_mx(
                             out=acc[:, j, :],
-                            lhsT=w2_codes[e, half][:, c, col * P : (col + 1) * P].bitcast(FP8X4),
-                            lhsT_scale=w2_scales[e, half][:, c, col * P : (col + 1) * P],
+                            lhsT=codes[:, c, m].bitcast(FP8X4),
+                            lhsT_scale=scales[:, c, m],
                             rhs=h1_codes[e][:, c, :].bitcast(FP8X4),
                             rhs_scale=h1_scales[e][:, c, :],
                             start=(c == 0),
                             stop=(c == PASSES - 1),
                         )
-                for j in range(2):
-                    col = pair * 2 + j
-                    row = e * HALVES + half
-                    nc.scalar.activation(
-                        out=h2T[e, half][:, col, :],
-                        in_=acc[:, j, :],
-                        func=SILU,
-                        bias=b2_cols[:, col, row : row + 1],
-                    )
+
+        def second_swish(e, half):
+            h2T[e, half] = h2_pool.tile([P, COLS, BATCH], F32, name="h2T")
+            row = e * HALVES + half
+            for col in range(COLS):
+                nc.scalar.activation(
+                    out=h2T[e, half][:, col, :],
+                    in_=mx_acc[e, half, col // 2][:, col % 2, :],
+                    func=SILU,
+                    bias=b2_cols[:, col, row : row + 1],
+                )
 
         def transpose_back(e, half):
             for s in range(ROW_SETS):
@@ -283,46 +332,66 @@ def tile_environvectorfield_pa_kernel(tc, u, W1, b1, W2, b2, out):
                 nc.sync.dma_start(out=out_rows[:, s, e, half * HALF : (half + 1) * HALF], in_=h2_sb[:])
 
         for half in range(HALVES):
-            new_grouped(0, half)
-        regroup_copy(w2_grouped[0, 0][:, 0, :, :], w2_start[0][:])
-        quantise_w2(0, 0, 0, 1)
-        regroup_copy(w2_grouped[0, 1][:, 0, :, :], w2_start[1][:])
-        regroup_copy(w2_grouped[0, 0][:, 1, :, :], w2_second[:, :, 0:HALF])
-        quantise_w2(0, 1, 0, 1)
-        regroup_copy(w2_grouped[0, 1][:, 1, :, :], w2_second[:, :, HALF:HIDDEN])
-        quantise_w2(0, 0, 1, 2)
-        quantise_w2(0, 1, 1, 2)
-        transpose_x(0)
-        for first in range(FIRST_AHEAD + 1):
-            first_layer(*divmod(first, PASSES))
-            regroup_h1(*divmod(first, PASSES), vector=(first < FIRST_AHEAD))
-        transpose_x(1)
-        for first in range(FIRST_AHEAD):
-            quantise_h1(*divmod(first, PASSES))
+            new_grouped(0, half * HALF)
+            new_mx(0, half * HALF)
+        regroup_start(0, 0)
+        quantise_start(0, 0)
+        regroup_start(0, 1)
+        regroup_start(1, 0)
+        quantise_start(0, 1)
+        regroup_start(1, 1)
+        quantise_start(1, 0)
+        quantise_start(1, 1)
+        transpose_x(0, 1)
+        transpose_b1()
+        first_matmuls(0, 0)
+        first_swish(0, 0)
+        transpose_x(1, ENVS_IN_BANK)
+        transpose_b2()
+        first_matmuls(0, 1)
+        first_swish(0, 1)
+        regroup_h1(0, 0)
+        quantise_h1(0, 0)
+        quantise_h1(0, 1)
+        for step in range(PASSES, FIRST_AHEAD):
+            first_matmuls(*divmod(step, PASSES))
+            first_swish(*divmod(step, PASSES))
+        first_matmuls(*divmod(FIRST_AHEAD, PASSES))
 
-        for i in range(1, STEPS + 2):
-            e, half = divmod(i, HALVES)
-            if HALVES <= i and e + LOAD_AHEAD < ENVS:
-                load_w2(e + LOAD_AHEAD, half)
-                if half == 0:
-                    load_w1(e + LOAD_AHEAD)
-            if 0 <= i - 2:
-                store(*divmod(i - 2, HALVES), on_vector={STEPS: (0, 1), STEPS + 1: (1,)}.get(i, ()))
-            if HALVES <= i < STEPS:
-                regroup_w2(e, half)
-                if i == FIRST_AHEAD:
-                    regroup_h1(*divmod(i, PASSES), scalar=False)
-                    quantise_h1(*divmod(i, PASSES))
-                if i + 1 < STEPS:
-                    regroup_h1(*divmod(i + 1, PASSES))
-                    if half == 0:
-                        quantise_h1(*divmod(i + 1, PASSES))
-                quantise_w2(e, half)
-                if i + 1 < STEPS and half == 1:
-                    quantise_h1(*divmod(i + 1, PASSES))
-            if i - 1 < STEPS:
-                second_layer(*divmod(i - 1, HALVES))
+        for i in range(STEPS + 2):
+            e_next, half_next = divmod(i + 1, HALVES)
+            if PASSES <= i + 1 and e_next + LOAD_AHEAD < ENVS:
+                if half_next == 0 and e_next + LOAD_AHEAD + 1 < ENVS:
+                    load_w1(e_next + LOAD_AHEAD + 1)
+                load_w2(e_next + LOAD_AHEAD, half_next)
+            if i + 2 < STEPS:
+                regroup_h1(*divmod(i + 2, PASSES), vector=False)
             if i + FIRST_AHEAD < STEPS:
-                first_layer(*divmod(i + FIRST_AHEAD, PASSES))
-            if i - 1 < STEPS:
+                first_swish(*divmod(i + FIRST_AHEAD, PASSES))
+            if i < STEPS:
+                second_matmuls(*divmod(i, HALVES))
+            if i < STEPS:
+                second_swish(*divmod(i, HALVES))
+            if i == 2:
+                transpose_x(ENVS_IN_BANK, ENVS)
+            if i + FIRST_AHEAD + 1 < STEPS:
+                first_matmuls(*divmod(i + FIRST_AHEAD + 1, PASSES))
+            if 1 <= i <= STEPS:
                 transpose_back(*divmod(i - 1, HALVES))
+            if HALVES <= i + 1 < STEPS:
+                todo = pieces(e_next, half_next)
+                for n0, width in todo:
+                    regroup_w2(e_next, n0, width)
+                if i + 2 < STEPS:
+                    regroup_h1(*divmod(i + 2, PASSES), scalar=False)
+                    if half_next == 0:
+                        quantise_h1(*divmod(i + 2, PASSES))
+                for n0, width in todo:
+                    quantise_w2(e_next, n0, width)
+                if i + 2 < STEPS and half_next == 1:
+                    quantise_h1(*divmod(i + 2, PASSES))
+            elif i + 2 < STEPS:
+                regroup_h1(*divmod(i + 2, PASSES), scalar=False)
+                quantise_h1(*divmod(i + 2, PASSES))
+            if 2 <= i:
+                store(*divmod(i - 2, HALVES), on_vector={STEPS - 1: (0, 1), STEPS: (0, 1), STEPS + 1: (1,)}.get(i, ()))

@@ -26,10 +26,9 @@ COLS = HALF // P
 STEPS = ENVS * HALVES
 RUN = 8
 LOAD_AHEAD = 2
-LAST_PIECES = 2
+LAST_WIDTHS = (256, 128, 128)
 FIRST_AHEAD = 3
 ENVS_IN_BANK = 4
-H1_SCALAR_COLS = 128
 
 FLOPS = 2 * ENVS * BATCH * HIDDEN * (D_IN + HIDDEN)
 
@@ -64,34 +63,38 @@ def tile_environvectorfield_pa_kernel(tc, u, W1, b1, W2, b2, out):
                 w2_raw[e] = raw_pool.tile([P, PASSES, PACK, HIDDEN], BF16, name="w2_raw")
             nc.sync.dma_start(out=w2_raw[e][:, c, :, :], in_=w2_rows(e, c))
 
-        start_pieces = [(0, 0, HALF), (0, HALF, HALF), (1, 0, HIDDEN)]
+        start_pieces = [(0, 0, HALF), (0, HALF, HALF), (1, 0, HALF), (1, HALF, HALF)]
         w2_start = [const.tile([P, PACK, w], BF16, name="w2_start_%d_%d" % (c, n0)) for c, n0, w in start_pieces]
         u_rows = u.rearrange("(p s e) d -> p s e d", s=ROW_SETS, e=ENVS)
-        u_sb = [
-            const.tile([P, ROW_SETS, ENVS_IN_BANK, D_IN], BF16, name="u_sb_%d" % g) for g in range(ENVS // ENVS_IN_BANK)
-        ]
+        u_sb = {}
 
-        def load_u(g):
-            nc.sync.dma_start(out=u_sb[g][:], in_=u_rows[:, :, g * ENVS_IN_BANK : (g + 1) * ENVS_IN_BANK, :])
+        def load_u(e0, e1):
+            tile = const.tile([P, ROW_SETS, e1 - e0, D_IN], BF16, name="u_sb_%d" % e0)
+            nc.sync.dma_start(out=tile[:], in_=u_rows[:, :, e0:e1, :])
+            for e in range(e0, e1):
+                u_sb[e] = tile[:, :, e - e0, :]
 
         def load_start(i):
             c, n0, width = start_pieces[i]
             nc.sync.dma_start(out=w2_start[i][:], in_=w2_rows(0, c)[:, :, n0 : n0 + width])
 
         bias_rows = const.tile([P, K_PASS], BF16, name="bias_rows")
-        nc.gpsimd.memset(bias_rows[:], 0.0)
+        for p0, p1 in ((2 * B_ROWS, P // 2), (P // 2, P)):
+            nc.vector.memset(bias_rows[p0:p1, :], 0.0)
         load_start(0)
-        load_u(0)
+        load_u(0, 1)
         nc.sync.dma_start(out=bias_rows[0:B_ROWS, :], in_=b1.rearrange("e (c n) -> (e c) n", n=K_PASS))
         nc.sync.dma_start(out=bias_rows[B_ROWS : 2 * B_ROWS, :], in_=b2.rearrange("e (c n) -> (e c) n", n=K_PASS))
         load_w1(0)
         load_start(1)
         load_start(2)
+        load_u(1, ENVS_IN_BANK)
+        load_start(3)
         load_w1(1)
         load_w2(1, 0)
-        load_w1(2)
         load_w2(1, 1)
-        load_u(1)
+        load_w1(2)
+        load_u(ENVS_IN_BANK, ENVS)
         load_w1(3)
         for c in range(PASSES):
             load_w2(2, c)
@@ -132,7 +135,7 @@ def tile_environvectorfield_pa_kernel(tc, u, W1, b1, W2, b2, out):
                 for s in range(ROW_SETS):
                     nc.tensor.transpose(
                         out=xT_ps[:, e - e0, s, :],
-                        in_=u_sb[e // ENVS_IN_BANK][:, s, e % ENVS_IN_BANK, :],
+                        in_=u_sb[e][:, s, :],
                         identity=ident_bf16[:],
                     )
             nc.scalar.copy(out=xT[:, e0:e1, :, :], in_=xT_ps[:, 0 : e1 - e0, :, :])
@@ -196,22 +199,14 @@ def tile_environvectorfield_pa_kernel(tc, u, W1, b1, W2, b2, out):
                         func=SILU,
                     )
 
-        def regroup_h1(e, c, vector=True, scalar=True):
+        def regroup_h1(e, c, copy=nc.scalar.copy):
             if c != 0:
                 return
-            if scalar:
-                h1_grouped[e, c] = h1_pool.tile([P, BATCH, PACK], BF16, name="h1_grouped", align_bytes=64)
-            split = BATCH - H1_SCALAR_COLS
-            shares = []
-            if vector:
-                shares.append((nc.vector.tensor_copy, 0, split))
-            if scalar:
-                shares.append((nc.scalar.copy, split, BATCH))
-            for copy, n0, n1 in shares:
-                copy(
-                    out=h1_grouped[e, c][:, n0:n1, :].rearrange("p (k i) t -> p k t i", i=RUN),
-                    in_=h1_bf16[e, c][:, :, n0:n1].rearrange("p t (k i) -> p k t i", i=RUN),
-                )
+            h1_grouped[e, c] = h1_pool.tile([P, BATCH, PACK], BF16, name="h1_grouped", align_bytes=64)
+            copy(
+                out=h1_grouped[e, c][:].rearrange("p (k i) t -> p k t i", i=RUN),
+                in_=h1_bf16[e, c][:].rearrange("p t (k i) -> p k t i", i=RUN),
+            )
 
         def quantise_h1(e, c):
             if c == 0:
@@ -256,11 +251,7 @@ def tile_environvectorfield_pa_kernel(tc, u, W1, b1, W2, b2, out):
             )
 
         def regroup_start(c, half):
-            if c == 0:
-                src = w2_start[half][:]
-            else:
-                src = w2_start[HALVES][:, :, half * HALF : (half + 1) * HALF]
-            regroup_copy(w2_grouped[0, half * HALF][:, c, :, :], src)
+            regroup_copy(w2_grouped[0, half * HALF][:, c, :, :], w2_start[c * HALVES + half][:])
 
         def quantise_start(c, half):
             nc.vector.quantize_mx(
@@ -270,9 +261,8 @@ def tile_environvectorfield_pa_kernel(tc, u, W1, b1, W2, b2, out):
             )
 
         def pieces(e, half):
-            count = LAST_PIECES if (e, half) == (ENVS - 1, HALVES - 1) else 1
-            width = HALF // count
-            return [(half * HALF + i * width, width) for i in range(count)]
+            widths = LAST_WIDTHS if (e, half) == (ENVS - 1, HALVES - 1) else (HALF,)
+            return [(half * HALF + sum(widths[:i]), width) for i, width in enumerate(widths)]
 
         h2T = {}
         h2_back = {}
@@ -311,6 +301,22 @@ def tile_environvectorfield_pa_kernel(tc, u, W1, b1, W2, b2, out):
                     bias=b2_cols[:, col, row : row + 1],
                 )
 
+        def transpose_back_last(e, half, pair):
+            h2_back[e, half, pair] = psum_back.tile([P, ROW_SETS, 2, P], F32, name="h2_back", tag="back")
+            for j in range(2):
+                for s in range(ROW_SETS):
+                    nc.tensor.transpose(
+                        out=h2_back[e, half, pair][:, s, j, :],
+                        in_=h2T[e, half][:, pair * 2 + j, s * P : (s + 1) * P],
+                        identity=ident_f32[:],
+                    )
+
+        def store_last(e, half, pair, copy):
+            h2_sb = out_pool.tile([P, ROW_SETS, 2 * P], F32, name="h2_sb")
+            copy(out=h2_sb[:], in_=h2_back[e, half, pair][:].rearrange("p s c n -> p s (c n)"))
+            n0 = half * HALF + pair * 2 * P
+            nc.sync.dma_start(out=out_rows[:, :, e, n0 : n0 + 2 * P], in_=h2_sb[:])
+
         def transpose_back(e, half):
             for s in range(ROW_SETS):
                 h2_back[e, half, s] = psum_back.tile([P, COLS, P], F32, name="h2_back", tag="back")
@@ -324,10 +330,9 @@ def tile_environvectorfield_pa_kernel(tc, u, W1, b1, W2, b2, out):
 
         out_rows = out.rearrange("(p s) e n -> p s e n", s=ROW_SETS)
 
-        def store(e, half, on_vector):
+        def store(e, half, copy):
             for s in range(ROW_SETS):
                 h2_sb = out_pool.tile([P, HALF], F32, name="h2_sb")
-                copy = nc.vector.tensor_copy if s in on_vector else nc.scalar.copy
                 copy(out=h2_sb[:], in_=h2_back[e, half, s][:].rearrange("p c n -> p (c n)"))
                 nc.sync.dma_start(out=out_rows[:, s, e, half * HALF : (half + 1) * HALF], in_=h2_sb[:])
 
@@ -346,11 +351,11 @@ def tile_environvectorfield_pa_kernel(tc, u, W1, b1, W2, b2, out):
         transpose_b1()
         first_matmuls(0, 0)
         first_swish(0, 0)
-        transpose_x(1, ENVS_IN_BANK)
-        transpose_b2()
         first_matmuls(0, 1)
         first_swish(0, 1)
-        regroup_h1(0, 0)
+        transpose_x(1, ENVS_IN_BANK)
+        transpose_b2()
+        regroup_h1(0, 0, copy=nc.vector.tensor_copy)
         quantise_h1(0, 0)
         quantise_h1(0, 1)
         for step in range(PASSES, FIRST_AHEAD):
@@ -358,40 +363,46 @@ def tile_environvectorfield_pa_kernel(tc, u, W1, b1, W2, b2, out):
             first_swish(*divmod(step, PASSES))
         first_matmuls(*divmod(FIRST_AHEAD, PASSES))
 
-        for i in range(STEPS + 2):
+        for i in range(STEPS - 1):
+            copies_first = i + FIRST_AHEAD >= STEPS
             e_next, half_next = divmod(i + 1, HALVES)
             if PASSES <= i + 1 and e_next + LOAD_AHEAD < ENVS:
                 if half_next == 0 and e_next + LOAD_AHEAD + 1 < ENVS:
                     load_w1(e_next + LOAD_AHEAD + 1)
                 load_w2(e_next + LOAD_AHEAD, half_next)
             if i + 2 < STEPS:
-                regroup_h1(*divmod(i + 2, PASSES), vector=False)
+                regroup_h1(*divmod(i + 2, PASSES))
             if i + FIRST_AHEAD < STEPS:
                 first_swish(*divmod(i + FIRST_AHEAD, PASSES))
-            if i < STEPS:
-                second_matmuls(*divmod(i, HALVES))
-            if i < STEPS:
-                second_swish(*divmod(i, HALVES))
-            if i == 2:
+            second_matmuls(*divmod(i, HALVES))
+            if copies_first:
+                store(*divmod(i - 2, HALVES), copy=nc.scalar.copy)
+            second_swish(*divmod(i, HALVES))
+            if i == 1:
                 transpose_x(ENVS_IN_BANK, ENVS)
             if i + FIRST_AHEAD + 1 < STEPS:
                 first_matmuls(*divmod(i + FIRST_AHEAD + 1, PASSES))
-            if 1 <= i <= STEPS:
+            if 1 <= i:
                 transpose_back(*divmod(i - 1, HALVES))
             if HALVES <= i + 1 < STEPS:
                 todo = pieces(e_next, half_next)
                 for n0, width in todo:
                     regroup_w2(e_next, n0, width)
                 if i + 2 < STEPS:
-                    regroup_h1(*divmod(i + 2, PASSES), scalar=False)
-                    if half_next == 0:
-                        quantise_h1(*divmod(i + 2, PASSES))
+                    quantise_h1(*divmod(i + 2, PASSES))
                 for n0, width in todo:
                     quantise_w2(e_next, n0, width)
-                if i + 2 < STEPS and half_next == 1:
-                    quantise_h1(*divmod(i + 2, PASSES))
             elif i + 2 < STEPS:
-                regroup_h1(*divmod(i + 2, PASSES), scalar=False)
                 quantise_h1(*divmod(i + 2, PASSES))
-            if 2 <= i:
-                store(*divmod(i - 2, HALVES), on_vector={STEPS - 1: (0, 1), STEPS: (0, 1), STEPS + 1: (1,)}.get(i, ()))
+            if 2 <= i and not copies_first:
+                store(*divmod(i - 2, HALVES), copy=nc.scalar.copy)
+
+        last = divmod(STEPS - 1, HALVES)
+        transpose_back(*divmod(STEPS - 2, HALVES))
+        second_matmuls(*last)
+        store(*divmod(STEPS - 3, HALVES), copy=nc.scalar.copy)
+        second_swish(*last)
+        store(*divmod(STEPS - 2, HALVES), copy=nc.vector.tensor_copy)
+        for pair, copy in enumerate((nc.vector.tensor_copy, nc.scalar.copy)):
+            transpose_back_last(*last, pair)
+            store_last(*last, pair, copy)

@@ -162,16 +162,20 @@ def tile_environvectorfield_pa_kernel(tc, u, W1, b1, W2, b2, out):
                         )
                 else:
                     acc = psum_hidden.tile([P, PACK, P], F32, name="hidden_acc")
+                    nc.tensor.matmul(
+                        out=acc[:],
+                        lhsT=ident_bf16[:],
+                        rhs=b1_bf16[:, :, row : row + 1].to_broadcast([P, PACK, P]),
+                        start=True,
+                        stop=False,
+                    )
                     for t in range(PACK):
                         nc.tensor.matmul(
                             out=acc[:, t, :],
-                            lhsT=ident_bf16[:],
-                            rhs=b1_bf16[:, t, row : row + 1].to_broadcast([P, P]),
-                            start=True,
-                            stop=False,
-                        )
-                        nc.tensor.matmul(
-                            out=acc[:, t, :], lhsT=w1_columns(e, c, t), rhs=xT[:, e, bank, :], start=False, stop=True
+                            lhsT=w1_columns(e, c, t),
+                            rhs=xT[:, e, bank, :],
+                            start=False,
+                            stop=(t == PACK - 1),
                         )
                 hidden_acc[e, c, bank] = acc
 
@@ -237,6 +241,11 @@ def tile_environvectorfield_pa_kernel(tc, u, W1, b1, W2, b2, out):
         def regroup_w2(e, n0, width=HALF):
             new_grouped(e, n0, width)
             regroup_copy(w2_grouped[e, n0][:], w2_raw[e][:, :, :, n0 : n0 + width])
+
+        def regroup_w2_pass(e, n0, c):
+            if c == 0:
+                new_grouped(e, n0)
+            regroup_copy(w2_grouped[e, n0][:, c, :, :], w2_raw[e][:, c, :, n0 : n0 + HALF])
 
         def new_mx(e, n0, width=HALF):
             w2_codes[e, n0] = w2_mx_pool.tile([P, PASSES, width], U32, name="w2_codes", align_bytes=64)
@@ -330,10 +339,10 @@ def tile_environvectorfield_pa_kernel(tc, u, W1, b1, W2, b2, out):
 
         out_rows = out.rearrange("(p s) e n -> p s e n", s=ROW_SETS)
 
-        def store(e, half, copy):
+        def store(e, half, copies):
             for s in range(ROW_SETS):
                 h2_sb = out_pool.tile([P, HALF], F32, name="h2_sb")
-                copy(out=h2_sb[:], in_=h2_back[e, half, s][:].rearrange("p c n -> p (c n)"))
+                copies[s](out=h2_sb[:], in_=h2_back[e, half, s][:].rearrange("p c n -> p (c n)"))
                 nc.sync.dma_start(out=out_rows[:, s, e, half * HALF : (half + 1) * HALF], in_=h2_sb[:])
 
         for half in range(HALVES):
@@ -376,7 +385,7 @@ def tile_environvectorfield_pa_kernel(tc, u, W1, b1, W2, b2, out):
                 first_swish(*divmod(i + FIRST_AHEAD, PASSES))
             second_matmuls(*divmod(i, HALVES))
             if copies_first:
-                store(*divmod(i - 2, HALVES), copy=nc.scalar.copy)
+                store(*divmod(i - 2, HALVES), copies=(nc.scalar.copy, nc.scalar.copy))
             second_swish(*divmod(i, HALVES))
             if i == 1:
                 transpose_x(ENVS_IN_BANK, ENVS)
@@ -386,23 +395,29 @@ def tile_environvectorfield_pa_kernel(tc, u, W1, b1, W2, b2, out):
                 transpose_back(*divmod(i - 1, HALVES))
             if HALVES <= i + 1 < STEPS:
                 todo = pieces(e_next, half_next)
-                for n0, width in todo:
+                if i == 1:
+                    for c in range(PASSES):
+                        regroup_w2_pass(e_next, todo[0][0], c)
+                        quantise_h1(1, c)
+                else:
+                    for n0, width in todo[:2]:
+                        regroup_w2(e_next, n0, width)
+                    if i + 2 < STEPS:
+                        quantise_h1(*divmod(i + 2, PASSES))
+                quantise_w2(e_next, *todo[0])
+                for n0, width in todo[2:]:
                     regroup_w2(e_next, n0, width)
-                if i + 2 < STEPS:
-                    quantise_h1(*divmod(i + 2, PASSES))
-                for n0, width in todo:
+                for n0, width in todo[1:]:
                     quantise_w2(e_next, n0, width)
-            elif i + 2 < STEPS:
-                quantise_h1(*divmod(i + 2, PASSES))
             if 2 <= i and not copies_first:
-                store(*divmod(i - 2, HALVES), copy=nc.scalar.copy)
+                store(*divmod(i - 2, HALVES), copies=(nc.scalar.copy, nc.scalar.copy))
 
         last = divmod(STEPS - 1, HALVES)
         transpose_back(*divmod(STEPS - 2, HALVES))
         second_matmuls(*last)
-        store(*divmod(STEPS - 3, HALVES), copy=nc.scalar.copy)
+        store(*divmod(STEPS - 3, HALVES), copies=(nc.scalar.copy, nc.vector.tensor_copy))
         second_swish(*last)
-        store(*divmod(STEPS - 2, HALVES), copy=nc.vector.tensor_copy)
+        store(*divmod(STEPS - 2, HALVES), copies=(nc.vector.tensor_copy, nc.vector.tensor_copy))
         for pair, copy in enumerate((nc.vector.tensor_copy, nc.scalar.copy)):
             transpose_back_last(*last, pair)
             store_last(*last, pair, copy)

from contextlib import ExitStack

import concourse.mybir as mybir
from concourse.masks import make_identity

BF16 = mybir.dt.bfloat16
F32 = mybir.dt.float32
U32 = mybir.dt.uint32
U8 = mybir.dt.uint8
FP8X4 = mybir.dt.float8_e4m3fn_x4
SILU = mybir.ActivationFunctionType.Silu

P = 128
PACK = 4
ENVS = 8
BATCH = 256
D_IN = 128
HIDDEN = 1024
K_PASS = P * PACK
PASSES = HIDDEN // K_PASS
B_ROWS = ENVS * PASSES
ROW_SETS = BATCH // P
HALF = 512
HALVES = HIDDEN // HALF
COLS = HALF // P
STEPS = ENVS * HALVES
RUN = 8
LOAD_AHEAD = 2
LAST_WIDTHS = (256, 128, 128)
FIRST_AHEAD = 3
ENVS_IN_BANK = 4

FLOPS = 2 * ENVS * BATCH * HIDDEN * (D_IN + HIDDEN)


def tile_environvectorfield_pa_kernel(tc, u, W1, b1, W2, b2, out):
    nc = tc.nc
    with ExitStack() as ctx:
        const = ctx.enter_context(tc.tile_pool(name="const", bufs=1))
        raw_pool = ctx.enter_context(tc.tile_pool(name="raw", bufs=LOAD_AHEAD + 2))
        grouped_pool = ctx.enter_context(tc.tile_pool(name="grouped", bufs=3))
        w2_mx_pool = ctx.enter_context(tc.tile_pool(name="w2_mx", bufs=3))
        h1_pool = ctx.enter_context(tc.tile_pool(name="h1", bufs=4))
        h1_mx_pool = ctx.enter_context(tc.tile_pool(name="h1_mx", bufs=3))
        h2_pool = ctx.enter_context(tc.tile_pool(name="h2", bufs=3))
        out_pool = ctx.enter_context(tc.tile_pool(name="out", bufs=6))
        psum_hidden = ctx.enter_context(tc.psum_pool(name="psum_hidden", bufs=2))
        psum_mx = ctx.enter_context(tc.psum_pool(name="psum_mx", bufs=2))
        psum_back = ctx.enter_context(tc.psum_pool(name="psum_back", bufs=4))
        ctx.enter_context(tc.manual_schedule())

        w1_sb = const.tile([P, ENVS, HIDDEN], BF16, name="w1_sb")
        w2_raw = {}

        def load_w1(e):
            nc.sync.dma_start(out=w1_sb[:, e, :], in_=W1[e])

        def w2_rows(e, c):
            return W2[e, c * K_PASS : (c + 1) * K_PASS, :].rearrange("(p t) n -> p t n", t=PACK)

        def load_w2(e, c):
            if c == 0:
                w2_raw[e] = raw_pool.tile([P, PASSES, PACK, HIDDEN], BF16, name="w2_raw")
            nc.sync.dma_start(out=w2_raw[e][:, c, :, :], in_=w2_rows(e, c))

        start_pieces = [(0, 0, HALF), (0, HALF, HALF), (1, 0, HALF), (1, HALF, HALF)]
        w2_start = [const.tile([P, PACK, w], BF16, name="w2_start_%d_%d" % (c, n0)) for c, n0, w in start_pieces]
        u_rows = u.rearrange("(p s e) d -> p s e d", s=ROW_SETS, e=ENVS)
        u_sb = {}

        def load_u(e0, e1):
            tile = const.tile([P, ROW_SETS, e1 - e0, D_IN], BF16, name="u_sb_%d" % e0)
            nc.sync.dma_start(out=tile[:], in_=u_rows[:, :, e0:e1, :])
            for e in range(e0, e1):
                u_sb[e] = tile[:, :, e - e0, :]

        def load_start(i):
            c, n0, width = start_pieces[i]
            nc.sync.dma_start(out=w2_start[i][:], in_=w2_rows(0, c)[:, :, n0 : n0 + width])

        bias_rows = const.tile([P, K_PASS], BF16, name="bias_rows")
        for p0, p1 in ((2 * B_ROWS, P // 2), (P // 2, P)):
            nc.vector.memset(bias_rows[p0:p1, :], 0.0)
        load_start(0)
        load_u(0, 1)
        nc.sync.dma_start(out=bias_rows[0:B_ROWS, :], in_=b1.rearrange("e (c n) -> (e c) n", n=K_PASS))
        nc.sync.dma_start(out=bias_rows[B_ROWS : 2 * B_ROWS, :], in_=b2.rearrange("e (c n) -> (e c) n", n=K_PASS))
        load_w1(0)
        load_start(1)
        load_start(2)
        load_u(1, ENVS_IN_BANK)
        load_start(3)
        load_w1(1)
        load_w2(1, 0)
        load_w2(1, 1)
        load_w1(2)
        load_u(ENVS_IN_BANK, ENVS)
        load_w1(3)
        for c in range(PASSES):
            load_w2(2, c)

        warm = const.tile([P, 1], F32, name="warm")
        nc.vector.memset(warm[:], 0.0)
        nc.scalar.activation(out=warm[:], in_=warm[:], func=SILU)

        ident_bf16 = const.tile([P, P], BF16, name="ident_bf16")
        make_identity(nc, ident_bf16[:])
        ident_f32 = const.tile([P, P], F32, name="ident_f32")
        make_identity(nc, ident_f32[:])

        b1_cols = const.tile([P, PACK, B_ROWS], F32, name="b1_cols")
        b1_bf16 = const.tile([P, PACK, B_ROWS], BF16, name="b1_bf16")
        b2_cols = const.tile([P, COLS, B_ROWS], F32, name="b2_cols")

        def transpose_b1():
            b1_ps = psum_back.tile([P, PACK, P], BF16, name="b1_ps", tag="back")
            for t in range(PACK):
                nc.tensor.transpose(out=b1_ps[:, t, :], in_=bias_rows[:, t::PACK], identity=ident_bf16[:])
            nc.scalar.copy(out=b1_cols[:], in_=b1_ps[:, :, 0:B_ROWS])
            nc.scalar.copy(out=b1_bf16[:], in_=b1_ps[:, :, 0:B_ROWS])

        def transpose_b2():
            b2_ps = psum_back.tile([P, COLS, P], BF16, name="b2_ps", tag="back")
            for col in range(COLS):
                nc.tensor.transpose(
                    out=b2_ps[:, col, :], in_=bias_rows[:, col * P : (col + 1) * P], identity=ident_bf16[:]
                )
            nc.scalar.copy(out=b2_cols[:], in_=b2_ps[:, :, B_ROWS : 2 * B_ROWS])

        xT = const.tile([P, ENVS, ROW_SETS, P], BF16, name="xT")

        def transpose_x(e0, e1):
            xT_ps = psum_back.tile([P, ENVS_IN_BANK, ROW_SETS, P], BF16, name="xT_ps", tag="back")
            for e in range(e0, e1):
                for s in range(ROW_SETS):
                    nc.tensor.transpose(
                        out=xT_ps[:, e - e0, s, :],
                        in_=u_sb[e][:, s, :],
                        identity=ident_bf16[:],
                    )
            nc.scalar.copy(out=xT[:, e0:e1, :, :], in_=xT_ps[:, 0 : e1 - e0, :, :])

        h1_bf16 = {}
        h1_grouped = {}
        h1_codes = {}
        h1_scales = {}

        def w1_columns(e, c, t):
            return w1_sb[:, e, c * K_PASS + t : (c + 1) * K_PASS : PACK]

        hidden_acc = {}

        def first_matmuls(e, c):
            row = e * PASSES + c
            for bank in range(2):
                if c == 0:
                    acc = psum_hidden.tile([P, 2, BATCH], F32, name="hidden_acc")
                    x_cols = xT[:, e, :, :].rearrange("d s p -> d (s p)")
                    for j in range(2):
                        nc.tensor.matmul(
                            out=acc[:, j, :], lhsT=w1_columns(e, c, bank * 2 + j), rhs=x_cols, start=True, stop=True
                        )
                else:
                    acc = psum_hidden.tile([P, PACK, P], F32, name="hidden_acc")
                    nc.tensor.matmul(
                        out=acc[:],
                        lhsT=ident_bf16[:],
                        rhs=b1_bf16[:, :, row : row + 1].to_broadcast([P, PACK, P]),
                        start=True,
                        stop=False,
                    )
                    for t in range(PACK):
                        nc.tensor.matmul(
                            out=acc[:, t, :],
                            lhsT=w1_columns(e, c, t),
                            rhs=xT[:, e, bank, :],
                            start=False,
                            stop=(t == PACK - 1),
                        )
                hidden_acc[e, c, bank] = acc

        def first_swish(e, c):
            row = e * PASSES + c
            if c == 0:
                h1_bf16[e, c] = h1_pool.tile([P, PACK, BATCH], BF16, name="h1_bf16")
            else:
                h1_grouped[e, c] = h1_pool.tile([P, BATCH, PACK], BF16, name="h1_grouped", align_bytes=64)
            for bank in range(2):
                acc = hidden_acc[e, c, bank]
                if c == 0:
                    for j in range(2):
                        t = bank * 2 + j
                        nc.scalar.activation(
                            out=h1_bf16[e, c][:, t, :],
                            in_=acc[:, j, :],
                            func=SILU,
                            bias=b1_cols[:, t, row : row + 1],
                        )
                else:
                    nc.scalar.activation(
                        out=h1_grouped[e, c][:, bank * P : (bank + 1) * P, :],
                        in_=acc[:].rearrange("p t n -> p n t"),
                        func=SILU,
                    )

        def regroup_h1(e, c, copy=nc.scalar.copy):
            if c != 0:
                return
            h1_grouped[e, c] = h1_pool.tile([P, BATCH, PACK], BF16, name="h1_grouped", align_bytes=64)
            copy(
                out=h1_grouped[e, c][:].rearrange("p (k i) t -> p k t i", i=RUN),
                in_=h1_bf16[e, c][:].rearrange("p t (k i) -> p k t i", i=RUN),
            )

        def quantise_h1(e, c):
            if c == 0:
                h1_codes[e] = h1_mx_pool.tile([P, PASSES, BATCH], U32, name="h1_codes", align_bytes=64)
                h1_scales[e] = h1_mx_pool.tile([P, PASSES, BATCH], U8, name="h1_scales", align_bytes=64)
            nc.vector.quantize_mx(
                out=h1_codes[e][:, c, :].bitcast(FP8X4),
                scales=h1_scales[e][:, c, :],
                in_=h1_grouped[e, c][:].rearrange("p w t -> p (w t)"),
            )

        w2_grouped = {}
        w2_codes = {}
        w2_scales = {}

        def regroup_copy(dst, src):
            if len(dst.shape) == 3:
                dst = dst.rearrange("p (k i) t -> p k t i", i=RUN)
                src = src.rearrange("p t (k i) -> p k t i", i=RUN)
            else:
                dst = dst.rearrange("p c (k i) t -> p c k t i", i=RUN)
                src = src.rearrange("p c t (k i) -> p c k t i", i=RUN)
            nc.vector.tensor_copy(out=dst, in_=src)

        def new_grouped(e, n0, width=HALF):
            w2_grouped[e, n0] = grouped_pool.tile([P, PASSES, width, PACK], BF16, name="w2_grouped", align_bytes=64)

        def regroup_w2(e, n0, width=HALF):
            new_grouped(e, n0, width)
            regroup_copy(w2_grouped[e, n0][:], w2_raw[e][:, :, :, n0 : n0 + width])

        def regroup_w2_pass(e, n0, c):
            if c == 0:
                new_grouped(e, n0)
            regroup_copy(w2_grouped[e, n0][:, c, :, :], w2_raw[e][:, c, :, n0 : n0 + HALF])

        def new_mx(e, n0, width=HALF):
            w2_codes[e, n0] = w2_mx_pool.tile([P, PASSES, width], U32, name="w2_codes", align_bytes=64)
            w2_scales[e, n0] = w2_mx_pool.tile([P, PASSES, width], U8, name="w2_scales", align_bytes=64)

        def quantise_w2(e, n0, width=HALF):
            new_mx(e, n0, width)
            nc.vector.quantize_mx(
                out=w2_codes[e, n0][:].rearrange("p c w -> p (c w)").bitcast(FP8X4),
                scales=w2_scales[e, n0][:].rearrange("p c w -> p (c w)"),
                in_=w2_grouped[e, n0][:].rearrange("p c w t -> p (c w t)"),
            )

        def regroup_start(c, half):
            regroup_copy(w2_grouped[0, half * HALF][:, c, :, :], w2_start[c * HALVES + half][:])

        def quantise_start(c, half):
            nc.vector.quantize_mx(
                out=w2_codes[0, half * HALF][:, c, :].bitcast(FP8X4),
                scales=w2_scales[0, half * HALF][:, c, :],
                in_=w2_grouped[0, half * HALF][:, c, :, :].rearrange("p w t -> p (w t)"),
            )

        def pieces(e, half):
            widths = LAST_WIDTHS if (e, half) == (ENVS - 1, HALVES - 1) else (HALF,)
            return [(half * HALF + sum(widths[:i]), width) for i, width in enumerate(widths)]

        h2T = {}
        h2_back = {}

        mx_acc = {}

        def second_matmuls(e, half):
            stationary = []
            for n0, width in pieces(e, half):
                for m0 in range(0, width, P):
                    stationary.append((w2_codes[e, n0], w2_scales[e, n0], slice(m0, m0 + P)))
            for pair in range(COLS // 2):
                acc = psum_mx.tile([P, 2, BATCH], F32, name="mx_acc")
                mx_acc[e, half, pair] = acc
                for j in range(2):
                    codes, scales, m = stationary[pair * 2 + j]
                    for c in range(PASSES):
                        nc.tensor.matmul_mx(
                            out=acc[:, j, :],
                            lhsT=codes[:, c, m].bitcast(FP8X4),
                            lhsT_scale=scales[:, c, m],
                            rhs=h1_codes[e][:, c, :].bitcast(FP8X4),
                            rhs_scale=h1_scales[e][:, c, :],
                            start=(c == 0),
                            stop=(c == PASSES - 1),
                        )

        def second_swish(e, half):
            h2T[e, half] = h2_pool.tile([P, COLS, BATCH], F32, name="h2T")
            row = e * HALVES + half
            for col in range(COLS):
                nc.scalar.activation(
                    out=h2T[e, half][:, col, :],
                    in_=mx_acc[e, half, col // 2][:, col % 2, :],
                    func=SILU,
                    bias=b2_cols[:, col, row : row + 1],
                )

        def transpose_back_last(e, half, pair):
            h2_back[e, half, pair] = psum_back.tile([P, ROW_SETS, 2, P], F32, name="h2_back", tag="back")
            for j in range(2):
                for s in range(ROW_SETS):
                    nc.tensor.transpose(
                        out=h2_back[e, half, pair][:, s, j, :],
                        in_=h2T[e, half][:, pair * 2 + j, s * P : (s + 1) * P],
                        identity=ident_f32[:],
                    )

        def store_last(e, half, pair, copy):
            h2_sb = out_pool.tile([P, ROW_SETS, 2 * P], F32, name="h2_sb")
            copy(out=h2_sb[:], in_=h2_back[e, half, pair][:].rearrange("p s c n -> p s (c n)"))
            n0 = half * HALF + pair * 2 * P
            nc.sync.dma_start(out=out_rows[:, :, e, n0 : n0 + 2 * P], in_=h2_sb[:])

        def transpose_back(e, half):
            for s in range(ROW_SETS):
                h2_back[e, half, s] = psum_back.tile([P, COLS, P], F32, name="h2_back", tag="back")
            for col in range(COLS):
                for s in range(ROW_SETS):
                    nc.tensor.transpose(
                        out=h2_back[e, half, s][:, col, :],
                        in_=h2T[e, half][:, col, s * P : (s + 1) * P],
                        identity=ident_f32[:],
                    )

        out_rows = out.rearrange("(p s) e n -> p s e n", s=ROW_SETS)

        def store(e, half, copies):
            for s in range(ROW_SETS):
                h2_sb = out_pool.tile([P, HALF], F32, name="h2_sb")
                copies[s](out=h2_sb[:], in_=h2_back[e, half, s][:].rearrange("p c n -> p (c n)"))
                nc.sync.dma_start(out=out_rows[:, s, e, half * HALF : (half + 1) * HALF], in_=h2_sb[:])

        for half in range(HALVES):
            new_grouped(0, half * HALF)
            new_mx(0, half * HALF)
        regroup_start(0, 0)
        quantise_start(0, 0)
        regroup_start(0, 1)
        regroup_start(1, 0)
        quantise_start(0, 1)
        regroup_start(1, 1)
        quantise_start(1, 0)
        quantise_start(1, 1)
        transpose_x(0, 1)
        transpose_b1()
        first_matmuls(0, 0)
        first_swish(0, 0)
        first_matmuls(0, 1)
        first_swish(0, 1)
        transpose_x(1, ENVS_IN_BANK)
        transpose_b2()
        regroup_h1(0, 0, copy=nc.vector.tensor_copy)
        quantise_h1(0, 0)
        quantise_h1(0, 1)
        for step in range(PASSES, FIRST_AHEAD):
            first_matmuls(*divmod(step, PASSES))
            first_swish(*divmod(step, PASSES))
        first_matmuls(*divmod(FIRST_AHEAD, PASSES))

        for i in range(STEPS - 1):
            copies_first = i + FIRST_AHEAD >= STEPS
            e_next, half_next = divmod(i + 1, HALVES)
            if PASSES <= i + 1 and e_next + LOAD_AHEAD < ENVS:
                if half_next == 0 and e_next + LOAD_AHEAD + 1 < ENVS:
                    load_w1(e_next + LOAD_AHEAD + 1)
                load_w2(e_next + LOAD_AHEAD, half_next)
            if i + 2 < STEPS:
                regroup_h1(*divmod(i + 2, PASSES))
            if i + FIRST_AHEAD < STEPS:
                first_swish(*divmod(i + FIRST_AHEAD, PASSES))
            second_matmuls(*divmod(i, HALVES))
            if copies_first:
                store(*divmod(i - 2, HALVES), copies=(nc.scalar.copy, nc.scalar.copy))
            second_swish(*divmod(i, HALVES))
            if i == 1:
                transpose_x(ENVS_IN_BANK, ENVS)
            if i + FIRST_AHEAD + 1 < STEPS:
                first_matmuls(*divmod(i + FIRST_AHEAD + 1, PASSES))
            if 1 <= i:
                transpose_back(*divmod(i - 1, HALVES))
            if HALVES <= i + 1 < STEPS:
                todo = pieces(e_next, half_next)
                if i == 1:
                    for c in range(PASSES):
                        regroup_w2_pass(e_next, todo[0][0], c)
                        quantise_h1(1, c)
                else:
                    for n0, width in todo[:2]:
                        regroup_w2(e_next, n0, width)
                    if i + 2 < STEPS:
                        quantise_h1(*divmod(i + 2, PASSES))
                quantise_w2(e_next, *todo[0])
                for n0, width in todo[2:]:
                    regroup_w2(e_next, n0, width)
                for n0, width in todo[1:]:
                    quantise_w2(e_next, n0, width)
            if 2 <= i and not copies_first:
                store(*divmod(i - 2, HALVES), copies=(nc.scalar.copy, nc.scalar.copy))

        last = divmod(STEPS - 1, HALVES)
        transpose_back(*divmod(STEPS - 2, HALVES))
        second_matmuls(*last)
        store(*divmod(STEPS - 3, HALVES), copies=(nc.scalar.copy, nc.vector.tensor_copy))
        second_swish(*last)
        store(*divmod(STEPS - 2, HALVES), copies=(nc.vector.tensor_copy, nc.vector.tensor_copy))
        for pair, copy in enumerate((nc.vector.tensor_copy, nc.scalar.copy)):
            transpose_back_last(*last, pair)
            store_last(*last, pair, copy)
